import numpy as np
import ml_dtypes


def mxq(x, axis, fmt="e4m3"):
    dtype, down = {"e4m3": (ml_dtypes.float8_e4m3fn, 7), "e5m2": (ml_dtypes.float8_e5m2, 14)}[fmt]
    v = np.moveaxis(np.asarray(x, np.float32).astype(ml_dtypes.bfloat16).astype(np.float64), axis, -1)
    blocks = v.reshape(v.shape[:-1] + (-1, 32))
    amax = np.abs(blocks).max(-1, keepdims=True)
    byte = np.maximum(np.where(amax > 0, np.frexp(amax)[1] - 1 + 127, 0) - down, 1)
    scale = np.exp2(byte - 127.0)
    codes = (blocks / scale).astype(np.float32).astype(dtype).astype(np.float64)
    return np.moveaxis((codes * scale).reshape(v.shape), -1, axis)


WIDE = False


def mx_kscale(k):
    if not WIDE:
        return np.ones(k)
    levels = np.array([20, -20, 10, -10, 0])
    a = np.random.permutation(np.resize(levels, k // 512 * 4)).reshape(k // 512, 4)
    idx = np.arange(k)
    return np.exp2(a[idx // 512, idx % 128 // 32])


BF16 = ml_dtypes.bfloat16


def bf(x):
    return np.asarray(x, np.float32).astype(BF16)


def f64(x):
    return np.asarray(x).astype(np.float64)


B, N, V = 2, 16, 16
D = 128
E = 128
O = 512
K = D * E


def setup_inputs():
    u = mx_kscale(O)
    node_embed = np.random.standard_normal((B, N, D))
    veh_fea = np.random.standard_normal((B, V, E))
    W = np.random.standard_normal((O, K)) * 0.008 / u[:, None]
    b = np.random.standard_normal(O) * 0.3
    g = np.random.standard_normal((B, N, V, O)) * np.exp2(np.random.randint(-12, 1, (B, N, V, 1))) * u
    return {"node_embed": bf(node_embed), "veh_fea": bf(veh_fea), "W": bf(W), "b": bf(b),
            "grad_out": bf(g)}


def reference(node_embed, veh_fea, W, b, grad_out):
    veh = f64(veh_fea)
    g = f64(grad_out)
    nb, nn, nv, no = g.shape
    ne = veh.shape[2]
    nd = f64(W).shape[1] // ne
    g2 = g.reshape(nb * nn * nv, no)
    gz = mxq(g2, 1, "e5m2") @ mxq(f64(W), 0, "e4m3")
    gz = gz.reshape(nb, nn, nv, nd, ne)
    return (gz * veh[:, None, :, None, :]).sum(axis=(2, 4))

@@ -1,0 +1,216 @@
+from contextlib import ExitStack
+
+import concourse.mybir as mybir
+from concourse.masks import make_identity
+
+FLOPS = 2 * 512 * 512 * 16384 + 2 * 512 * 16384
+
+BF16 = mybir.dt.bfloat16
+F32 = mybir.dt.float32
+U32 = mybir.dt.uint32
+U8 = mybir.dt.uint8
+E4 = mybir.dt.float8_e4m3fn_x4
+E5 = mybir.dt.float8_e5m2_x4
+MULT = mybir.AluOpType.mult
+ADD = mybir.AluOpType.add
+AX = mybir.AxisListType.X
+
+P = 128
+UNITS = 32
+BANKS = 4 * UNITS
+AHEAD = 4
+LAG = 1
+V_SHARE = 14
+CHUNKS = [1, 1] + [2] * 15
+RAW_BUFS = 5
+ACC_SPLIT = [0, 64, 112, 128]
+
+
+def tile_bilinearpooling_kernel(tc, node_embed, veh_fea, W, b, grad_out, out):
+    nc = tc.nc
+    with ExitStack() as ctx:
+        const = ctx.enter_context(tc.tile_pool(name="const", bufs=1))
+        rawp = ctx.enter_context(tc.tile_pool(name="rawp", bufs=RAW_BUFS))
+        grp = ctx.enter_context(tc.tile_pool(name="grp", bufs=3))
+        wp = ctx.enter_context(tc.tile_pool(name="wp", bufs=4))
+        gtp = ctx.enter_context(tc.tile_pool(name="gtp", bufs=6))
+        work = ctx.enter_context(tc.tile_pool(name="work", bufs=2))
+        psb = ctx.enter_context(tc.psum_pool(name="psb", bufs=5))
+        psk = ctx.enter_context(tc.psum_pool(name="psk", bufs=1))
+        ctx.enter_context(tc.manual_schedule())
+
+        Wv = W.rearrange("(q p) c -> p q c", p=P)
+        chunk_first = [sum(CHUNKS[:c]) for c in range(len(CHUNKS))]
+        unit_chunk = {}
+        for c in range(len(CHUNKS)):
+            for h in range(CHUNKS[c]):
+                unit_chunk[chunk_first[c] + h] = (c, h)
+        raws = {}
+
+        def load(c):
+            if c >= len(CHUNKS):
+                return
+            raw = rawp.tile([P, 4, 1024], BF16, tag="raw")
+            width = 512 * CHUNKS[c]
+            c0 = 512 * chunk_first[c]
+            nc.sync.dma_start(out=raw[:, :, 0:width], in_=Wv[:, :, c0 : c0 + width])
+            raws[c] = raw
+
+        vehpad = const.tile([P, P], BF16)
+        nc.vector.memset(vehpad[:], 0.0)
+        nc.sync.dma_start(out=vehpad[0:32, :], in_=veh_fea.rearrange("b v e -> (b v) e"))
+        x_sb = const.tile([P, 4, 512], BF16)
+        gview = grad_out.rearrange("b n (t v) o -> v (b n) t o", v=4)
+        for v4 in range(4):
+            nc.sync.dma_start(out=x_sb[32 * v4 : 32 * v4 + 32, :, :], in_=gview[v4])
+        for c in range(RAW_BUFS):
+            load(c)
+
+        ident = const.tile([P, P], BF16)
+        make_identity(nc, ident[:])
+
+        sel = const.tile([P, P], F32)
+        nc.vector.memset(sel[:], 0.0)
+        mask = const.tile([P, 8], F32)
+        nc.vector.tensor_reduce(
+            out=mask[:], in_=ident[:].rearrange("m (j n) -> m j n", n=16), axis=AX, op=ADD
+        )
+        nc.vector.tensor_reduce(
+            out=sel[:, 0:32], in_=ident[:].rearrange("m (q c) -> m c q", q=4), axis=AX, op=ADD
+        )
+
+        vT_ps = psb.tile([P, P], BF16, tag="pb")
+        nc.tensor.transpose(vT_ps[:], vehpad[:], ident[:])
+        ymov = const.tile([P, 4, 8], F32)
+        nc.vector.tensor_copy(
+            out=ymov[:].rearrange("e t (v b) -> e t v b", b=2),
+            in_=vT_ps[:, 0:32].rearrange("e (b t v) -> e t v b", b=2, t=4, v=4),
+        )
+
+        gg = const.tile([P, 4, P, 4], BF16, align_bytes=64)
+        for t in range(4):
+            xt = psb.tile([P, 4, P], BF16, tag="pb")
+            for q in range(4):
+                nc.tensor.transpose(xt[:, q, :], x_sb[:, t, P * q : P * q + P], ident[:])
+            if t % 2 == 0:
+                nc.vector.tensor_copy(out=gg[:, t, :, :], in_=xt[:].rearrange("p q m -> p m q"))
+            else:
+                nc.scalar.copy(out=gg[:, t, :, :], in_=xt[:].rearrange("p q m -> p m q"))
+        gw = const.tile([P, 512], U32, align_bytes=64)
+        gs = const.tile([P, 512], U8, align_bytes=64)
+        nc.vector.quantize_mx(
+            out=gw[:].bitcast(E5), scales=gs[:], in_=gg[:].rearrange("p a m q -> p (a m q)")
+        )
+
+        sums = const.tile([P, P], F32)
+        accs = [psk.tile([P, 512], F32, name="acc%d" % a) for a in range(len(ACC_SPLIT) - 1)]
+
+        grs = {}
+        wws = {}
+        pbs = {}
+        gts = {}
+
+        def regroup(u):
+            if u >= UNITS:
+                return
+            c, h = unit_chunk[u]
+            raw = raws[c]
+            gr = grp.tile([P, 512, 4], BF16, tag="gr", align_bytes=64)
+            nc.vector.tensor_copy(
+                out=gr[:].rearrange("p (c i) q -> p c q i", i=4),
+                in_=raw[:, :, 512 * h : 512 * h + 512].rearrange("p q (c i) -> p c q i", i=4),
+            )
+            grs[u] = gr
+            if h == CHUNKS[c] - 1:
+                load(c + RAW_BUFS)
+
+        def quantise(u):
+            if u >= UNITS:
+                return
+            ww = wp.tile([P, 512], U32, tag="ww", align_bytes=64)
+            ws = wp.tile([P, 512], U8, tag="ws", align_bytes=64)
+            nc.vector.quantize_mx(
+                out=ww[:].bitcast(E4), scales=ws[:], in_=grs[u][:].rearrange("p w q -> p (w q)")
+            )
+            wws[u] = (ww, ws)
+
+        def mx_pass(j):
+            if j >= BANKS:
+                return
+            u, dd = divmod(j, 4)
+            ww, ws = wws[u]
+            pb = psb.tile([P, 512], F32, tag="pb")
+            nc.tensor.matmul_mx(
+                out=pb[:],
+                lhsT=ww[:, P * dd : P * dd + P].bitcast(E4),
+                lhsT_scale=ws[:, P * dd : P * dd + P],
+                rhs=gw[:].bitcast(E5),
+                rhs_scale=gs[:],
+                start=True,
+                stop=True,
+            )
+            pbs[j] = pb
+
+        def leave(j):
+            u, dd = divmod(j, 4)
+            gt = gtp.tile([P, 512], F32, tag="gt")
+            on_vector = dd == 3 and (u + 1) * V_SHARE // UNITS > u * V_SHARE // UNITS
+            if on_vector:
+                nc.vector.tensor_copy(out=gt[:], in_=pbs[j][:])
+            else:
+                nc.scalar.copy(out=gt[:], in_=pbs[j][:])
+            gts[j] = gt
+
+        def extract(a):
+            first = ACC_SPLIT[a]
+            count = ACC_SPLIT[a + 1] - first
+            prod = work.tile([P, 64, 8], F32, tag="prod")
+            nc.vector.tensor_tensor(
+                out=prod[:, 0:count, :],
+                in0=accs[a][:, 0 : 8 * count].rearrange("m (s j) -> m s j", j=8),
+                in1=mask[:].unsqueeze(1).to_broadcast([P, count, 8]),
+                op=MULT,
+            )
+            nc.vector.tensor_reduce(
+                out=sums[:, first : first + count], in_=prod[:, 0:count, :], axis=AX, op=ADD
+            )
+
+        def contract(j):
+            if j < 0:
+                return
+            a = max([x for x in range(len(ACC_SPLIT) - 1) if ACC_SPLIT[x] <= j])
+            s = j - ACC_SPLIT[a]
+            for t in range(4):
+                nc.tensor.matmul(
+                    accs[a][:, 8 * s : 8 * s + 8],
+                    lhsT=gts[j][:, P * t : P * t + P],
+                    rhs=ymov[:, t, :],
+                    start=(t == 0),
+                    stop=(t == 3),
+                )
+            if j + 1 == ACC_SPLIT[a + 1]:
+                extract(a)
+
+        regroup(0)
+        regroup(1)
+        quantise(0)
+        regroup(2)
+        quantise(1)
+        for j in range(AHEAD):
+            mx_pass(j)
+        for j in range(BANKS):
+            if j % 4 == 0:
+                regroup(j // 4 + 3)
+                quantise(j // 4 + 2)
+            mx_pass(j + AHEAD)
+            leave(j)
+            contract(j - LAG)
+        res = psb.tile([P, P], F32, tag="pb")
+        early = ACC_SPLIT[-2]
+        nc.tensor.matmul(res[:, 0:early], lhsT=sel[:], rhs=sums[:, 0:early], start=True, stop=True)
+        for j in range(BANKS - LAG, BANKS):
+            contract(j)
+        nc.tensor.matmul(res[:, early:P], lhsT=sel[:], rhs=sums[:, early:P], start=True, stop=True)
+        res_sb = const.tile([P, P], F32)
+        nc.vector.tensor_copy(out=res_sb[:], in_=res[:])
+        nc.sync.dma_start(out=out.rearrange("b n d -> (b n) d"), in_=res_sb[0:32, :])

@@ -13,16 +13,20 @@ E4 = mybir.dt.float8_e4m3fn_x4
 E5 = mybir.dt.float8_e5m2_x4
 MULT = mybir.AluOpType.mult
 ADD = mybir.AluOpType.add
+SUB = mybir.AluOpType.subtract
 AX = mybir.AxisListType.X
 
 P = 128
 UNITS = 32
 BANKS = 4 * UNITS
-AHEAD = 4
-LAG = 1
-V_SHARE = 14
+AHEAD = 3
+G_COLS = 384
+V_COLS = 0
+LEAD_G = 4
+LEAD_R = 3
+LEAD_Q = 2
 CHUNKS = [1, 1] + [2] * 15
-RAW_BUFS = 5
+RAW_BUFS = 6
 ACC_SPLIT = [0, 64, 112, 128]
 
 
@@ -31,7 +35,7 @@ def tile_bilinearpooling_kernel(tc, node_embed, veh_fea, W, b, grad_out, out):
     with ExitStack() as ctx:
         const = ctx.enter_context(tc.tile_pool(name="const", bufs=1))
         rawp = ctx.enter_context(tc.tile_pool(name="rawp", bufs=RAW_BUFS))
-        grp = ctx.enter_context(tc.tile_pool(name="grp", bufs=3))
+        grp = ctx.enter_context(tc.tile_pool(name="grp", bufs=LEAD_G + 1))
         wp = ctx.enter_context(tc.tile_pool(name="wp", bufs=4))
         gtp = ctx.enter_context(tc.tile_pool(name="gtp", bufs=6))
         work = ctx.enter_context(tc.tile_pool(name="work", bufs=2))
@@ -81,7 +85,7 @@ def tile_bilinearpooling_kernel(tc, node_embed, veh_fea, W, b, grad_out, out):
 
         vT_ps = psb.tile([P, P], BF16, tag="pb")
         nc.tensor.transpose(vT_ps[:], vehpad[:], ident[:])
-        ymov = const.tile([P, 4, 8], F32)
+        ymov = const.tile([P, 4, 8], BF16)
         nc.vector.tensor_copy(
             out=ymov[:].rearrange("e t (v b) -> e t v b", b=2),
             in_=vT_ps[:, 0:32].rearrange("e (b t v) -> e t v b", b=2, t=4, v=4),
@@ -108,19 +112,40 @@ def tile_bilinearpooling_kernel(tc, node_embed, veh_fea, W, b, grad_out, out):
         grs = {}
         wws = {}
         pbs = {}
-        gts = {}
+        his = {}
+        los = {}
 
-        def regroup(u):
+        def views(u, lo_col, hi_col):
+            c, h = unit_chunk[u]
+            dst = grs[u][:, lo_col:hi_col, :].rearrange("p (c i) q -> p c q i", i=4)
+            src = raws[c][:, :, 512 * h + lo_col : 512 * h + hi_col].rearrange(
+                "p q (c i) -> p c q i", i=4
+            )
+            return dst, src
+
+        def regroup_g(u):
             if u >= UNITS:
                 return
+            grs[u] = grp.tile([P, 512, 4], BF16, tag="gr", name="gr", align_bytes=64)
+            if G_COLS > 0:
+                dst, src = views(u, 0, G_COLS)
+                nc.gpsimd.tensor_scalar(
+                    out=dst, in0=src, scalar1=1.0, scalar2=0.0, op0=MULT, op1=ADD
+                )
+
+        def regroup_v(u):
+            if u >= UNITS or V_COLS == 0:
+                return
+            dst, src = views(u, G_COLS, G_COLS + V_COLS)
+            nc.vector.tensor_copy(out=dst, in_=src)
+
+        def regroup_s(u):
+            if u >= UNITS:
+                return
+            if G_COLS + V_COLS < 512:
+                dst, src = views(u, G_COLS + V_COLS, 512)
+                nc.scalar.copy(out=dst, in_=src)
             c, h = unit_chunk[u]
-            raw = raws[c]
-            gr = grp.tile([P, 512, 4], BF16, tag="gr", align_bytes=64)
-            nc.vector.tensor_copy(
-                out=gr[:].rearrange("p (c i) q -> p c q i", i=4),
-                in_=raw[:, :, 512 * h : 512 * h + 512].rearrange("p q (c i) -> p c q i", i=4),
-            )
-            grs[u] = gr
             if h == CHUNKS[c] - 1:
                 load(c + RAW_BUFS)
 
@@ -151,15 +176,17 @@ def tile_bilinearpooling_kernel(tc, node_embed, veh_fea, W, b, grad_out, out):
             )
             pbs[j] = pb
 
-        def leave(j):
-            u, dd = divmod(j, 4)
-            gt = gtp.tile([P, 512], F32, tag="gt")
-            on_vector = dd == 3 and (u + 1) * V_SHARE // UNITS > u * V_SHARE // UNITS
-            if on_vector:
-                nc.vector.tensor_copy(out=gt[:], in_=pbs[j][:])
-            else:
-                nc.scalar.copy(out=gt[:], in_=pbs[j][:])
-            gts[j] = gt
+        def high_part(j):
+            hi = gtp.tile([P, 512], BF16, tag="hi")
+            nc.scalar.copy(out=hi[:], in_=pbs[j][:])
+            his[j] = hi
+
+        def low_part(j):
+            if j < 0 or j >= BANKS:
+                return
+            lo = gtp.tile([P, 512], BF16, tag="lo")
+            nc.vector.tensor_tensor(out=lo[:], in0=pbs[j][:], in1=his[j][:], op=SUB)
+            los[j] = lo
 
         def extract(a):
             first = ACC_SPLIT[a]
@@ -176,40 +203,52 @@ def tile_bilinearpooling_kernel(tc, node_embed, veh_fea, W, b, grad_out, out):
             )
 
         def contract(j):
-            if j < 0:
+            if j < 0 or j >= BANKS:
                 return
             a = max([x for x in range(len(ACC_SPLIT) - 1) if ACC_SPLIT[x] <= j])
             s = j - ACC_SPLIT[a]
             for t in range(4):
-                nc.tensor.matmul(
-                    accs[a][:, 8 * s : 8 * s + 8],
-                    lhsT=gts[j][:, P * t : P * t + P],
-                    rhs=ymov[:, t, :],
-                    start=(t == 0),
-                    stop=(t == 3),
-                )
+                for part in (his[j], los[j]):
+                    nc.tensor.matmul(
+                        accs[a][:, 8 * s : 8 * s + 8],
+                        lhsT=part[:, P * t : P * t + P],
+                        rhs=ymov[:, t, :],
+                        start=(t == 0 and part is his[j]),
+                        stop=(t == 3 and part is los[j]),
+                    )
             if j + 1 == ACC_SPLIT[a + 1]:
                 extract(a)
 
-        regroup(0)
-        regroup(1)
-        quantise(0)
-        regroup(2)
-        quantise(1)
+        for u in range(LEAD_G):
+            regroup_g(u)
+        for u in range(LEAD_R):
+            regroup_v(u)
+            regroup_s(u)
+        for u in range(LEAD_Q):
+            quantise(u)
         for j in range(AHEAD):
             mx_pass(j)
-        for j in range(BANKS):
-            if j % 4 == 0:
-                regroup(j // 4 + 3)
-                quantise(j // 4 + 2)
-            mx_pass(j + AHEAD)
-            leave(j)
-            contract(j - LAG)
-        res = psb.tile([P, P], F32, tag="pb")
+        res = None
         early = ACC_SPLIT[-2]
-        nc.tensor.matmul(res[:, 0:early], lhsT=sel[:], rhs=sums[:, 0:early], start=True, stop=True)
-        for j in range(BANKS - LAG, BANKS):
-            contract(j)
+        for j in range(BANKS + 2):
+            u = j // 4
+            if j < BANKS:
+                mx_pass(j + AHEAD)
+                high_part(j)
+            low_part(j - 1)
+            if j < BANKS and j % 4 == 0:
+                regroup_g(u + LEAD_G)
+            if j < BANKS and j % 4 == 1:
+                regroup_v(u + LEAD_R)
+                regroup_s(u + LEAD_R)
+            if j < BANKS and j % 4 == 2:
+                quantise(u + LEAD_Q)
+            if j == BANKS:
+                res = psb.tile([P, P], F32, tag="pb")
+                nc.tensor.matmul(
+                    res[:, 0:early], lhsT=sel[:], rhs=sums[:, 0:early], start=True, stop=True
+                )
+            contract(j - 2)
         nc.tensor.matmul(res[:, early:P], lhsT=sel[:], rhs=sums[:, early:P], start=True, stop=True)
         res_sb = const.tile([P, P], F32)
         nc.vector.tensor_copy(out=res_sb[:], in_=res[:])

@@ -17,16 +17,16 @@ SUB = mybir.AluOpType.subtract
 AX = mybir.AxisListType.X
 
 P = 128
-UNITS = 32
-BANKS = 4 * UNITS
+BATCHES = 16
+PER = 8
+BANKS = PER * BATCHES
 AHEAD = 3
-G_COLS = 384
-V_COLS = 0
-LEAD_G = 4
-LEAD_R = 3
-LEAD_Q = 2
-CHUNKS = [1, 1] + [2] * 15
-RAW_BUFS = 6
+G_COLS = 768
+G_PIECES = 2
+S_PIECES = 2
+S_AT = [3, 6]
+Q_AT = 2
+RAW_BUFS = 5
 ACC_SPLIT = [0, 64, 112, 128]
 
 
@@ -35,8 +35,8 @@ def tile_bilinearpooling_kernel(tc, node_embed, veh_fea, W, b, grad_out, out):
     with ExitStack() as ctx:
         const = ctx.enter_context(tc.tile_pool(name="const", bufs=1))
         rawp = ctx.enter_context(tc.tile_pool(name="rawp", bufs=RAW_BUFS))
-        grp = ctx.enter_context(tc.tile_pool(name="grp", bufs=LEAD_G + 1))
-        wp = ctx.enter_context(tc.tile_pool(name="wp", bufs=4))
+        grp = ctx.enter_context(tc.tile_pool(name="grp", bufs=2))
+        wp = ctx.enter_context(tc.tile_pool(name="wp", bufs=3))
         gtp = ctx.enter_context(tc.tile_pool(name="gtp", bufs=6))
         work = ctx.enter_context(tc.tile_pool(name="work", bufs=2))
         psb = ctx.enter_context(tc.psum_pool(name="psb", bufs=5))
@@ -44,21 +44,19 @@ def tile_bilinearpooling_kernel(tc, node_embed, veh_fea, W, b, grad_out, out):
         ctx.enter_context(tc.manual_schedule())
 
         Wv = W.rearrange("(q p) c -> p q c", p=P)
-        chunk_first = [sum(CHUNKS[:c]) for c in range(len(CHUNKS))]
-        unit_chunk = {}
-        for c in range(len(CHUNKS)):
-            for h in range(CHUNKS[c]):
-                unit_chunk[chunk_first[c] + h] = (c, h)
         raws = {}
 
-        def load(c):
-            if c >= len(CHUNKS):
+        def load(n, parts):
+            if n >= BATCHES:
                 return
             raw = rawp.tile([P, 4, 1024], BF16, tag="raw")
-            width = 512 * CHUNKS[c]
-            c0 = 512 * chunk_first[c]
-            nc.sync.dma_start(out=raw[:, :, 0:width], in_=Wv[:, :, c0 : c0 + width])
-            raws[c] = raw
+            step = 1024 // parts
+            for k in range(parts):
+                nc.sync.dma_start(
+                    out=raw[:, :, step * k : step * k + step],
+                    in_=Wv[:, :, 1024 * n + step * k : 1024 * n + step * k + step],
+                )
+            raws[n] = raw
 
         vehpad = const.tile([P, P], BF16)
         nc.vector.memset(vehpad[:], 0.0)
@@ -67,8 +65,9 @@ def tile_bilinearpooling_kernel(tc, node_embed, veh_fea, W, b, grad_out, out):
         gview = grad_out.rearrange("b n (t v) o -> v (b n) t o", v=4)
         for v4 in range(4):
             nc.sync.dma_start(out=x_sb[32 * v4 : 32 * v4 + 32, :, :], in_=gview[v4])
-        for c in range(RAW_BUFS):
-            load(c)
+        load(0, 2)
+        for n in range(1, RAW_BUFS):
+            load(n, 1)
 
         ident = const.tile([P, P], BF16)
         make_identity(nc, ident[:])
@@ -115,55 +114,60 @@ def tile_bilinearpooling_kernel(tc, node_embed, veh_fea, W, b, grad_out, out):
         his = {}
         los = {}
 
-        def views(u, lo_col, hi_col):
-            c, h = unit_chunk[u]
-            dst = grs[u][:, lo_col:hi_col, :].rearrange("p (c i) q -> p c q i", i=4)
-            src = raws[c][:, :, 512 * h + lo_col : 512 * h + hi_col].rearrange(
-                "p q (c i) -> p c q i", i=4
-            )
+        def views(n, lo_col, hi_col):
+            dst = grs[n][:, lo_col:hi_col, :].rearrange("p (c i) q -> p c q i", i=4)
+            src = raws[n][:, :, lo_col:hi_col].rearrange("p q (c i) -> p c q i", i=4)
             return dst, src
 
-        def regroup_g(u):
-            if u >= UNITS:
-                return
-            grs[u] = grp.tile([P, 512, 4], BF16, tag="gr", name="gr", align_bytes=64)
-            if G_COLS > 0:
-                dst, src = views(u, 0, G_COLS)
+        def new_group(n):
+            grs[n] = grp.tile([P, 1024, 4], BF16, tag="gr", name="gr", align_bytes=64)
+
+        def regroup(n, engine, lo_col, hi_col):
+            dst, src = views(n, lo_col, hi_col)
+            if engine == "g":
                 nc.gpsimd.tensor_scalar(
                     out=dst, in0=src, scalar1=1.0, scalar2=0.0, op0=MULT, op1=ADD
                 )
-
-        def regroup_v(u):
-            if u >= UNITS or V_COLS == 0:
-                return
-            dst, src = views(u, G_COLS, G_COLS + V_COLS)
-            nc.vector.tensor_copy(out=dst, in_=src)
-
-        def regroup_s(u):
-            if u >= UNITS:
-                return
-            if G_COLS + V_COLS < 512:
-                dst, src = views(u, G_COLS + V_COLS, 512)
+            elif engine == "v":
+                nc.vector.tensor_copy(out=dst, in_=src)
+            else:
                 nc.scalar.copy(out=dst, in_=src)
-            c, h = unit_chunk[u]
-            if h == CHUNKS[c] - 1:
-                load(c + RAW_BUFS)
 
-        def quantise(u):
-            if u >= UNITS:
+        def regroup_g(n):
+            if n >= BATCHES:
                 return
-            ww = wp.tile([P, 512], U32, tag="ww", align_bytes=64)
-            ws = wp.tile([P, 512], U8, tag="ws", align_bytes=64)
+            new_group(n)
+            step = G_COLS // G_PIECES
+            for k in range(G_PIECES):
+                regroup(n, "g", step * k, step * k + step)
+
+        def regroup_s(n, k):
+            if n >= BATCHES:
+                return
+            step = (1024 - G_COLS) // S_PIECES
+            regroup(n, "s", G_COLS + step * k, G_COLS + step * k + step)
+            if k == S_PIECES - 1:
+                load(n + RAW_BUFS, 1)
+
+        def quantise(n, lo_col, hi_col):
+            if n >= BATCHES:
+                return
+            if n not in wws:
+                ww = wp.tile([P, 1024], U32, tag="ww", align_bytes=64)
+                ws = wp.tile([P, 1024], U8, tag="ws", align_bytes=64)
+                wws[n] = (ww, ws)
+            ww, ws = wws[n]
             nc.vector.quantize_mx(
-                out=ww[:].bitcast(E4), scales=ws[:], in_=grs[u][:].rearrange("p w q -> p (w q)")
+                out=ww[:, lo_col:hi_col].bitcast(E4),
+                scales=ws[:, lo_col:hi_col],
+                in_=grs[n][:, lo_col:hi_col, :].rearrange("p w q -> p (w q)"),
             )
-            wws[u] = (ww, ws)
 
         def mx_pass(j):
             if j >= BANKS:
                 return
-            u, dd = divmod(j, 4)
-            ww, ws = wws[u]
+            n, dd = divmod(j, PER)
+            ww, ws = wws[n]
             pb = psb.tile([P, 512], F32, tag="pb")
             nc.tensor.matmul_mx(
                 out=pb[:],
@@ -219,30 +223,34 @@ def tile_bilinearpooling_kernel(tc, node_embed, veh_fea, W, b, grad_out, out):
             if j + 1 == ACC_SPLIT[a + 1]:
                 extract(a)
 
-        for u in range(LEAD_G):
-            regroup_g(u)
-        for u in range(LEAD_R):
-            regroup_v(u)
-            regroup_s(u)
-        for u in range(LEAD_Q):
-            quantise(u)
+        new_group(0)
+        regroup(0, "v", 0, 512)
+        regroup(0, "g", 512, 768)
+        regroup(0, "s", 768, 1024)
+        load(RAW_BUFS, 1)
+        quantise(0, 0, 512)
+        new_group(1)
+        regroup(1, "g", 0, 384)
+        regroup(1, "s", 768, 1024)
+        quantise(0, 512, 1024)
+        regroup(1, "v", 384, 768)
+        load(RAW_BUFS + 1, 1)
         for j in range(AHEAD):
             mx_pass(j)
         res = None
         early = ACC_SPLIT[-2]
         for j in range(BANKS + 2):
-            u = j // 4
+            n, dd = divmod(j, PER)
             if j < BANKS:
                 mx_pass(j + AHEAD)
                 high_part(j)
             low_part(j - 1)
-            if j < BANKS and j % 4 == 0:
-                regroup_g(u + LEAD_G)
-            if j < BANKS and j % 4 == 1:
-                regroup_v(u + LEAD_R)
-                regroup_s(u + LEAD_R)
-            if j < BANKS and j % 4 == 2:
-                quantise(u + LEAD_Q)
+            if j < BANKS and dd == 0:
+                regroup_g(n + 2)
+            if j < BANKS and dd == Q_AT:
+                quantise(n + 1, 0, 1024)
+            if j < BANKS and dd in S_AT:
+                regroup_s(n + 2, S_AT.index(dd))
             if j == BANKS:
                 res = psb.tile([P, P], F32, tag="pb")
                 nc.tensor.matmul(

@@ -26,6 +26,8 @@ G_PIECES = 2
 S_PIECES = 2
 S_AT = [3, 6]
 Q_AT = 2
+G_LOW = [5]
+G_LAG = 6
 RAW_BUFS = 5
 ACC_SPLIT = [0, 64, 112, 128]
 
@@ -39,6 +41,7 @@ def tile_bilinearpooling_kernel(tc, node_embed, veh_fea, W, b, grad_out, out):
         wp = ctx.enter_context(tc.tile_pool(name="wp", bufs=3))
         gtp = ctx.enter_context(tc.tile_pool(name="gtp", bufs=6))
         work = ctx.enter_context(tc.tile_pool(name="work", bufs=2))
+        fullp = ctx.enter_context(tc.tile_pool(name="fullp", bufs=3))
         psb = ctx.enter_context(tc.psum_pool(name="psb", bufs=5))
         psk = ctx.enter_context(tc.psum_pool(name="psk", bufs=1))
         ctx.enter_context(tc.manual_schedule())
@@ -113,6 +116,7 @@ def tile_bilinearpooling_kernel(tc, node_embed, veh_fea, W, b, grad_out, out):
         pbs = {}
         his = {}
         los = {}
+        done = [0] * (len(ACC_SPLIT) - 1)
 
         def views(n, lo_col, hi_col):
             dst = grs[n][:, lo_col:hi_col, :].rearrange("p (c i) q -> p c q i", i=4)
@@ -180,13 +184,25 @@ def tile_bilinearpooling_kernel(tc, node_embed, veh_fea, W, b, grad_out, out):
             )
             pbs[j] = pb
 
+        def by_gpsimd(j):
+            return 0 <= j < BANKS - PER and j % PER in G_LOW
+
         def high_part(j):
+            if by_gpsimd(j):
+                full = fullp.tile([P, 512], F32, tag="full")
+                nc.scalar.copy(out=full[:], in_=pbs[j][:])
+                top = full[:].bitcast(BF16).rearrange("p (c two) -> p c two", two=2)[:, :, 1]
+                lo = fullp.tile([P, 512], BF16, tag="glo")
+                nc.gpsimd.tensor_tensor(out=lo[:], in0=full[:], in1=top, op=SUB)
+                his[j] = top
+                los[j] = lo
+                return
             hi = gtp.tile([P, 512], BF16, tag="hi")
             nc.scalar.copy(out=hi[:], in_=pbs[j][:])
             his[j] = hi
 
         def low_part(j):
-            if j < 0 or j >= BANKS:
+            if j < 0 or j >= BANKS or by_gpsimd(j):
                 return
             lo = gtp.tile([P, 512], BF16, tag="lo")
             nc.vector.tensor_tensor(out=lo[:], in0=pbs[j][:], in1=his[j][:], op=SUB)
@@ -212,15 +228,16 @@ def tile_bilinearpooling_kernel(tc, node_embed, veh_fea, W, b, grad_out, out):
             a = max([x for x in range(len(ACC_SPLIT) - 1) if ACC_SPLIT[x] <= j])
             s = j - ACC_SPLIT[a]
             for t in range(4):
-                for part in (his[j], los[j]):
+                for k, part in enumerate((his[j], los[j])):
                     nc.tensor.matmul(
                         accs[a][:, 8 * s : 8 * s + 8],
                         lhsT=part[:, P * t : P * t + P],
                         rhs=ymov[:, t, :],
-                        start=(t == 0 and part is his[j]),
-                        stop=(t == 3 and part is los[j]),
+                        start=(t == 0 and k == 0),
+                        stop=(t == 3 and k == 1),
                     )
-            if j + 1 == ACC_SPLIT[a + 1]:
+            done[a] += 1
+            if done[a] == ACC_SPLIT[a + 1] - ACC_SPLIT[a]:
                 extract(a)
 
         new_group(0)
@@ -256,7 +273,10 @@ def tile_bilinearpooling_kernel(tc, node_embed, veh_fea, W, b, grad_out, out):
                 nc.tensor.matmul(
                     res[:, 0:early], lhsT=sel[:], rhs=sums[:, 0:early], start=True, stop=True
                 )
-            contract(j - 2)
+            if not by_gpsimd(j - 2):
+                contract(j - 2)
+            if by_gpsimd(j - G_LAG):
+                contract(j - G_LAG)
         nc.tensor.matmul(res[:, early:P], lhsT=sel[:], rhs=sums[:, early:P], start=True, stop=True)
         res_sb = const.tile([P, P], F32)
         nc.vector.tensor_copy(out=res_sb[:], in_=res[:])

@@ -21,10 +21,10 @@ BATCHES = 16
 PER = 8
 BANKS = PER * BATCHES
 AHEAD = 3
-G_COLS = 768
+G_COLS = 640
 G_PIECES = 2
-S_PIECES = 2
-S_AT = [3, 6]
+S_PIECES = 3
+S_AT = [1, 3, 6]
 Q_AT = 2
 G_LOW = [5]
 G_LAG = 6
@@ -130,7 +130,12 @@ def tile_bilinearpooling_kernel(tc, node_embed, veh_fea, W, b, grad_out, out):
             dst, src = views(n, lo_col, hi_col)
             if engine == "g":
                 nc.gpsimd.tensor_scalar(
-                    out=dst, in0=src, scalar1=1.0, scalar2=0.0, op0=MULT, op1=ADD
+                    out=grs[n][:, lo_col:hi_col, :],
+                    in0=raws[n][:, :, lo_col:hi_col].rearrange("p q c -> p c q"),
+                    scalar1=1.0,
+                    scalar2=0.0,
+                    op0=MULT,
+                    op1=ADD,
                 )
             elif engine == "v":
                 nc.vector.tensor_copy(out=dst, in_=src)

@@ -26,8 +26,6 @@ G_PIECES = 2
 S_PIECES = 3
 S_AT = [1, 3, 6]
 Q_AT = 2
-G_LOW = [5]
-G_LAG = 6
 RAW_BUFS = 5
 ACC_SPLIT = [0, 64, 112, 128]
 
@@ -41,7 +39,6 @@ def tile_bilinearpooling_kernel(tc, node_embed, veh_fea, W, b, grad_out, out):
         wp = ctx.enter_context(tc.tile_pool(name="wp", bufs=3))
         gtp = ctx.enter_context(tc.tile_pool(name="gtp", bufs=6))
         work = ctx.enter_context(tc.tile_pool(name="work", bufs=2))
-        fullp = ctx.enter_context(tc.tile_pool(name="fullp", bufs=3))
         psb = ctx.enter_context(tc.psum_pool(name="psb", bufs=5))
         psk = ctx.enter_context(tc.psum_pool(name="psk", bufs=1))
         ctx.enter_context(tc.manual_schedule())
@@ -116,7 +113,6 @@ def tile_bilinearpooling_kernel(tc, node_embed, veh_fea, W, b, grad_out, out):
         pbs = {}
         his = {}
         los = {}
-        done = [0] * (len(ACC_SPLIT) - 1)
 
         def views(n, lo_col, hi_col):
             dst = grs[n][:, lo_col:hi_col, :].rearrange("p (c i) q -> p c q i", i=4)
@@ -130,12 +126,7 @@ def tile_bilinearpooling_kernel(tc, node_embed, veh_fea, W, b, grad_out, out):
             dst, src = views(n, lo_col, hi_col)
             if engine == "g":
                 nc.gpsimd.tensor_scalar(
-                    out=grs[n][:, lo_col:hi_col, :],
-                    in0=raws[n][:, :, lo_col:hi_col].rearrange("p q c -> p c q"),
-                    scalar1=1.0,
-                    scalar2=0.0,
-                    op0=MULT,
-                    op1=ADD,
+                    out=dst, in0=src, scalar1=1.0, scalar2=0.0, op0=MULT, op1=ADD
                 )
             elif engine == "v":
                 nc.vector.tensor_copy(out=dst, in_=src)
@@ -189,25 +180,13 @@ def tile_bilinearpooling_kernel(tc, node_embed, veh_fea, W, b, grad_out, out):
             )
             pbs[j] = pb
 
-        def by_gpsimd(j):
-            return 0 <= j < BANKS - PER and j % PER in G_LOW
-
         def high_part(j):
-            if by_gpsimd(j):
-                full = fullp.tile([P, 512], F32, tag="full")
-                nc.scalar.copy(out=full[:], in_=pbs[j][:])
-                top = full[:].bitcast(BF16).rearrange("p (c two) -> p c two", two=2)[:, :, 1]
-                lo = fullp.tile([P, 512], BF16, tag="glo")
-                nc.gpsimd.tensor_tensor(out=lo[:], in0=full[:], in1=top, op=SUB)
-                his[j] = top
-                los[j] = lo
-                return
             hi = gtp.tile([P, 512], BF16, tag="hi")
             nc.scalar.copy(out=hi[:], in_=pbs[j][:])
             his[j] = hi
 
         def low_part(j):
-            if j < 0 or j >= BANKS or by_gpsimd(j):
+            if j < 0 or j >= BANKS:
                 return
             lo = gtp.tile([P, 512], BF16, tag="lo")
             nc.vector.tensor_tensor(out=lo[:], in0=pbs[j][:], in1=his[j][:], op=SUB)
@@ -233,16 +212,15 @@ def tile_bilinearpooling_kernel(tc, node_embed, veh_fea, W, b, grad_out, out):
             a = max([x for x in range(len(ACC_SPLIT) - 1) if ACC_SPLIT[x] <= j])
             s = j - ACC_SPLIT[a]
             for t in range(4):
-                for k, part in enumerate((his[j], los[j])):
+                for part in (his[j], los[j]):
                     nc.tensor.matmul(
                         accs[a][:, 8 * s : 8 * s + 8],
                         lhsT=part[:, P * t : P * t + P],
                         rhs=ymov[:, t, :],
-                        start=(t == 0 and k == 0),
-                        stop=(t == 3 and k == 1),
+                        start=(t == 0 and part is his[j]),
+                        stop=(t == 3 and part is los[j]),
                     )
-            done[a] += 1
-            if done[a] == ACC_SPLIT[a + 1] - ACC_SPLIT[a]:
+            if j + 1 == ACC_SPLIT[a + 1]:
                 extract(a)
 
         new_group(0)
@@ -278,10 +256,7 @@ def tile_bilinearpooling_kernel(tc, node_embed, veh_fea, W, b, grad_out, out):
                 nc.tensor.matmul(
                     res[:, 0:early], lhsT=sel[:], rhs=sums[:, 0:early], start=True, stop=True
                 )
-            if not by_gpsimd(j - 2):
-                contract(j - 2)
-            if by_gpsimd(j - G_LAG):
-                contract(j - G_LAG)
+            contract(j - 2)
         nc.tensor.matmul(res[:, early:P], lhsT=sel[:], rhs=sums[:, early:P], start=True, stop=True)
         res_sb = const.tile([P, P], F32)
         nc.vector.tensor_copy(out=res_sb[:], in_=res[:])

from contextlib import ExitStack

import concourse.mybir as mybir
from concourse.masks import make_identity

FLOPS = 2 * 512 * 512 * 16384 + 2 * 512 * 16384

BF16 = mybir.dt.bfloat16
F32 = mybir.dt.float32
U32 = mybir.dt.uint32
U8 = mybir.dt.uint8
E4 = mybir.dt.float8_e4m3fn_x4
E5 = mybir.dt.float8_e5m2_x4
MULT = mybir.AluOpType.mult
ADD = mybir.AluOpType.add
SUB = mybir.AluOpType.subtract
AX = mybir.AxisListType.X

P = 128
BATCHES = 16
PER = 8
BANKS = PER * BATCHES
AHEAD = 3
G_COLS = 640
G_PIECES = 2
S_PIECES = 3
S_AT = [1, 3, 6]
Q_AT = 2
RAW_BUFS = 5
ACC_SPLIT = [0, 64, 112, 128]


def tile_bilinearpooling_kernel(tc, node_embed, veh_fea, W, b, grad_out, out):
    nc = tc.nc
    with ExitStack() as ctx:
        const = ctx.enter_context(tc.tile_pool(name="const", bufs=1))
        rawp = ctx.enter_context(tc.tile_pool(name="rawp", bufs=RAW_BUFS))
        grp = ctx.enter_context(tc.tile_pool(name="grp", bufs=2))
        wp = ctx.enter_context(tc.tile_pool(name="wp", bufs=3))
        gtp = ctx.enter_context(tc.tile_pool(name="gtp", bufs=6))
        work = ctx.enter_context(tc.tile_pool(name="work", bufs=2))
        psb = ctx.enter_context(tc.psum_pool(name="psb", bufs=5))
        psk = ctx.enter_context(tc.psum_pool(name="psk", bufs=1))
        ctx.enter_context(tc.manual_schedule())

        Wv = W.rearrange("(q p) c -> p q c", p=P)
        raws = {}

        def load(n, parts):
            if n >= BATCHES:
                return
            raw = rawp.tile([P, 4, 1024], BF16, tag="raw")
            step = 1024 // parts
            for k in range(parts):
                nc.sync.dma_start(
                    out=raw[:, :, step * k : step * k + step],
                    in_=Wv[:, :, 1024 * n + step * k : 1024 * n + step * k + step],
                )
            raws[n] = raw

        vehpad = const.tile([P, P], BF16)
        nc.vector.memset(vehpad[:], 0.0)
        nc.sync.dma_start(out=vehpad[0:32, :], in_=veh_fea.rearrange("b v e -> (b v) e"))
        x_sb = const.tile([P, 4, 512], BF16)
        gview = grad_out.rearrange("b n (t v) o -> v (b n) t o", v=4)
        for v4 in range(4):
            nc.sync.dma_start(out=x_sb[32 * v4 : 32 * v4 + 32, :, :], in_=gview[v4])
        load(0, 2)
        for n in range(1, RAW_BUFS):
            load(n, 1)

        ident = const.tile([P, P], BF16)
        make_identity(nc, ident[:])

        sel = const.tile([P, P], F32)
        nc.vector.memset(sel[:], 0.0)
        mask = const.tile([P, 8], F32)
        nc.vector.tensor_reduce(
            out=mask[:], in_=ident[:].rearrange("m (j n) -> m j n", n=16), axis=AX, op=ADD
        )
        nc.vector.tensor_reduce(
            out=sel[:, 0:32], in_=ident[:].rearrange("m (q c) -> m c q", q=4), axis=AX, op=ADD
        )

        vT_ps = psb.tile([P, P], BF16, tag="pb")
        nc.tensor.transpose(vT_ps[:], vehpad[:], ident[:])
        ymov = const.tile([P, 4, 8], BF16)
        nc.vector.tensor_copy(
            out=ymov[:].rearrange("e t (v b) -> e t v b", b=2),
            in_=vT_ps[:, 0:32].rearrange("e (b t v) -> e t v b", b=2, t=4, v=4),
        )

        gg = const.tile([P, 4, P, 4], BF16, align_bytes=64)
        for t in range(4):
            xt = psb.tile([P, 4, P], BF16, tag="pb")
            for q in range(4):
                nc.tensor.transpose(xt[:, q, :], x_sb[:, t, P * q : P * q + P], ident[:])
            if t % 2 == 0:
                nc.vector.tensor_copy(out=gg[:, t, :, :], in_=xt[:].rearrange("p q m -> p m q"))
            else:
                nc.scalar.copy(out=gg[:, t, :, :], in_=xt[:].rearrange("p q m -> p m q"))
        gw = const.tile([P, 512], U32, align_bytes=64)
        gs = const.tile([P, 512], U8, align_bytes=64)
        nc.vector.quantize_mx(
            out=gw[:].bitcast(E5), scales=gs[:], in_=gg[:].rearrange("p a m q -> p (a m q)")
        )

        sums = const.tile([P, P], F32)
        accs = [psk.tile([P, 512], F32, name="acc%d" % a) for a in range(len(ACC_SPLIT) - 1)]

        grs = {}
        wws = {}
        pbs = {}
        his = {}
        los = {}

        def views(n, lo_col, hi_col):
            dst = grs[n][:, lo_col:hi_col, :].rearrange("p (c i) q -> p c q i", i=4)
            src = raws[n][:, :, lo_col:hi_col].rearrange("p q (c i) -> p c q i", i=4)
            return dst, src

        def new_group(n):
            grs[n] = grp.tile([P, 1024, 4], BF16, tag="gr", name="gr", align_bytes=64)

        def regroup(n, engine, lo_col, hi_col):
            dst, src = views(n, lo_col, hi_col)
            if engine == "g":
                nc.gpsimd.tensor_scalar(
                    out=dst, in0=src, scalar1=1.0, scalar2=0.0, op0=MULT, op1=ADD
                )
            elif engine == "v":
                nc.vector.tensor_copy(out=dst, in_=src)
            else:
                nc.scalar.copy(out=dst, in_=src)

        def regroup_g(n):
            if n >= BATCHES:
                return
            new_group(n)
            step = G_COLS // G_PIECES
            for k in range(G_PIECES):
                regroup(n, "g", step * k, step * k + step)

        def regroup_s(n, k):
            if n >= BATCHES:
                return
            step = (1024 - G_COLS) // S_PIECES
            regroup(n, "s", G_COLS + step * k, G_COLS + step * k + step)
            if k == S_PIECES - 1:
                load(n + RAW_BUFS, 1)

        def quantise(n, lo_col, hi_col):
            if n >= BATCHES:
                return
            if n not in wws:
                ww = wp.tile([P, 1024], U32, tag="ww", align_bytes=64)
                ws = wp.tile([P, 1024], U8, tag="ws", align_bytes=64)
                wws[n] = (ww, ws)
            ww, ws = wws[n]
            nc.vector.quantize_mx(
                out=ww[:, lo_col:hi_col].bitcast(E4),
                scales=ws[:, lo_col:hi_col],
                in_=grs[n][:, lo_col:hi_col, :].rearrange("p w q -> p (w q)"),
            )

        def mx_pass(j):
            if j >= BANKS:
                return
            n, dd = divmod(j, PER)
            ww, ws = wws[n]
            pb = psb.tile([P, 512], F32, tag="pb")
            nc.tensor.matmul_mx(
                out=pb[:],
                lhsT=ww[:, P * dd : P * dd + P].bitcast(E4),
                lhsT_scale=ws[:, P * dd : P * dd + P],
                rhs=gw[:].bitcast(E5),
                rhs_scale=gs[:],
                start=True,
                stop=True,
            )
            pbs[j] = pb

        def high_part(j):
            hi = gtp.tile([P, 512], BF16, tag="hi")
            nc.scalar.copy(out=hi[:], in_=pbs[j][:])
            his[j] = hi

        def low_part(j):
            if j < 0 or j >= BANKS:
                return
            lo = gtp.tile([P, 512], BF16, tag="lo")
            nc.vector.tensor_tensor(out=lo[:], in0=pbs[j][:], in1=his[j][:], op=SUB)
            los[j] = lo

        def extract(a):
            first = ACC_SPLIT[a]
            count = ACC_SPLIT[a + 1] - first
            prod = work.tile([P, 64, 8], F32, tag="prod")
            nc.vector.tensor_tensor(
                out=prod[:, 0:count, :],
                in0=accs[a][:, 0 : 8 * count].rearrange("m (s j) -> m s j", j=8),
                in1=mask[:].unsqueeze(1).to_broadcast([P, count, 8]),
                op=MULT,
            )
            nc.vector.tensor_reduce(
                out=sums[:, first : first + count], in_=prod[:, 0:count, :], axis=AX, op=ADD
            )

        def contract(j):
            if j < 0 or j >= BANKS:
                return
            a = max([x for x in range(len(ACC_SPLIT) - 1) if ACC_SPLIT[x] <= j])
            s = j - ACC_SPLIT[a]
            for t in range(4):
                for part in (his[j], los[j]):
                    nc.tensor.matmul(
                        accs[a][:, 8 * s : 8 * s + 8],
                        lhsT=part[:, P * t : P * t + P],
                        rhs=ymov[:, t, :],
                        start=(t == 0 and part is his[j]),
                        stop=(t == 3 and part is los[j]),
                    )
            if j + 1 == ACC_SPLIT[a + 1]:
                extract(a)

        new_group(0)
        regroup(0, "v", 0, 512)
        regroup(0, "g", 512, 768)
        regroup(0, "s", 768, 1024)
        load(RAW_BUFS, 1)
        quantise(0, 0, 512)
        new_group(1)
        regroup(1, "g", 0, 384)
        regroup(1, "s", 768, 1024)
        quantise(0, 512, 1024)
        regroup(1, "v", 384, 768)
        load(RAW_BUFS + 1, 1)
        for j in range(AHEAD):
            mx_pass(j)
        res = None
        early = ACC_SPLIT[-2]
        for j in range(BANKS + 2):
            n, dd = divmod(j, PER)
            if j < BANKS:
                mx_pass(j + AHEAD)
                high_part(j)
            low_part(j - 1)
            if j < BANKS and dd == 0:
                regroup_g(n + 2)
            if j < BANKS and dd == Q_AT:
                quantise(n + 1, 0, 1024)
            if j < BANKS and dd in S_AT:
                regroup_s(n + 2, S_AT.index(dd))
            if j == BANKS:
                res = psb.tile([P, P], F32, tag="pb")
                nc.tensor.matmul(
                    res[:, 0:early], lhsT=sel[:], rhs=sums[:, 0:early], start=True, stop=True
                )
            contract(j - 2)
        nc.tensor.matmul(res[:, early:P], lhsT=sel[:], rhs=sums[:, early:P], start=True, stop=True)
        res_sb = const.tile([P, P], F32)
        nc.vector.tensor_copy(out=res_sb[:], in_=res[:])
        nc.sync.dma_start(out=out.rearrange("b n d -> (b n) d"), in_=res_sb[0:32, :])
